import numpy as np
import ml_dtypes


def mxq(x, axis, fmt="e4m3"):
    dtype, down = {"e4m3": (ml_dtypes.float8_e4m3fn, 7), "e5m2": (ml_dtypes.float8_e5m2, 14)}[fmt]
    v = np.moveaxis(np.asarray(x, np.float32).astype(ml_dtypes.bfloat16).astype(np.float64), axis, -1)
    blocks = v.reshape(v.shape[:-1] + (-1, 32))
    amax = np.abs(blocks).max(-1, keepdims=True)
    byte = np.maximum(np.where(amax > 0, np.frexp(amax)[1] - 1 + 127, 0) - down, 1)
    scale = np.exp2(byte - 127.0)
    codes = (blocks / scale).astype(np.float32).astype(dtype).astype(np.float64)
    return np.moveaxis((codes * scale).reshape(v.shape), -1, axis)


WIDE = False


def mx_kscale(k):
    if not WIDE:
        return np.ones(k)
    levels = np.array([10, -10, 5, -5, 0])
    a = np.random.permutation(np.resize(levels, k // 512 * 4)).reshape(k // 512, 4)
    idx = np.arange(k)
    return np.exp2(a[idx // 512, idx % 128 // 32])


BF16 = ml_dtypes.bfloat16


def bf(x):
    return np.asarray(x, np.float32).astype(BF16)


def f64(x):
    return np.asarray(x).astype(np.float64)


B, D, F, R, HT, S = 2, 128, 512, 128, 1, 1024


def silu(v):
    return v / (1.0 + np.exp(-v))


def setup_inputs():
    t = mx_kscale(F)
    mlp = silu(np.random.standard_normal((B, F, HT, S))) * np.random.standard_normal((B, F, HT, S))
    return {
        "mlp": bf(mlp * t[None, :, None, None]),
        "down_snapped": bf(np.random.standard_normal((D, F)) * 1.5 / np.sqrt(F) / t[None, :]),
        "down_scale_A": bf(np.random.standard_normal((D, R))),
        "down_scale_B": bf(np.random.standard_normal((R, F)) / np.sqrt(R)),
    }


def reference(mlp, down_snapped, down_scale_A, down_scale_B):
    down_eff = f64(down_snapped) * (f64(down_scale_A) @ f64(down_scale_B))
    out = mxq(down_eff, 1, "e4m3") @ mxq(f64(mlp).reshape(B, F, HT * S), 1, "e4m3")
    return out.reshape(B, D, HT, S)

@@ -1,0 +1,118 @@
+from contextlib import ExitStack
+
+import concourse.mybir as mybir
+from concourse.masks import make_identity
+
+BF16 = mybir.dt.bfloat16
+F32 = mybir.dt.float32
+U32 = mybir.dt.uint32
+U8 = mybir.dt.uint8
+FP8X4 = mybir.dt.float8_e4m3fn_x4
+
+P = 128
+PACK = 4
+BATCH, CHANNELS, D_OUT, RANK, WIDTH = 2, 512, 128, 128, 1024
+N_TILE = 512
+VECTOR_COLS = N_TILE * 5 // 8
+RUN = 4
+
+FLOPS = 2 * BATCH * WIDTH * CHANNELS * D_OUT + 2 * D_OUT * RANK * CHANNELS
+
+
+def regroup(copy, grouped, raw, cols):
+    copy(
+        out=grouped[:, cols, :].rearrange("p (c i) j -> p c j i", i=RUN),
+        in_=raw[:, :, cols].rearrange("p j (c i) -> p c j i", i=RUN),
+    )
+
+
+def tile_ffnwithscales_pb_s_kernel(
+    tc, mlp, down_snapped, down_scale_A, down_scale_B, out
+):
+    nc = tc.nc
+    mlp_by_word = mlp.rearrange("b (p j) h w -> b p j (h w)", j=PACK)
+    out_rows = out.rearrange("b o h w -> b o (h w)")
+    tiles = [(b, slice(n, n + N_TILE)) for b in range(BATCH) for n in range(0, WIDTH, N_TILE)]
+
+    with ExitStack() as ctx:
+        weights = ctx.enter_context(tc.tile_pool(name="weights", bufs=1))
+        weights_psum = ctx.enter_context(tc.psum_pool(name="weights_psum", bufs=1))
+        stream = ctx.enter_context(tc.tile_pool(name="stream", bufs=len(tiles)))
+        acc_psum = ctx.enter_context(tc.psum_pool(name="acc_psum", bufs=len(tiles)))
+
+        a_sb = weights.tile([D_OUT, RANK], BF16)
+        nc.scalar.dma_start(out=a_sb[:], in_=down_scale_A)
+        snapped_sb = weights.tile([D_OUT, CHANNELS], BF16)
+        nc.scalar.dma_start(out=snapped_sb[:], in_=down_snapped)
+        b_sb = weights.tile([RANK, CHANNELS], BF16)
+        nc.scalar.dma_start(out=b_sb[:], in_=down_scale_B)
+
+        raws = []
+        for b, cols in tiles:
+            raw = stream.tile([P, PACK, N_TILE], BF16)
+            nc.sync.dma_start(out=raw[:], in_=mlp_by_word[b, :, :, cols])
+            raws.append(raw)
+
+        identity = weights.tile([P, P], BF16)
+        make_identity(nc, identity[:])
+
+        a_t_psum = weights_psum.tile([RANK, D_OUT], BF16)
+        nc.tensor.transpose(a_t_psum[:], a_sb[:], identity[:])
+        a_t = weights.tile([RANK, D_OUT], BF16)
+        nc.vector.tensor_copy(out=a_t[:], in_=a_t_psum[:])
+
+        snapped_by_j = snapped_sb[:].rearrange("o (p j) -> o j p", j=PACK)
+        snapped_t_psum = weights_psum.tile([P, PACK, D_OUT], BF16)
+        for j in range(PACK):
+            nc.tensor.transpose(snapped_t_psum[:, j, :], snapped_by_j[:, j, :], identity[:])
+        snapped_t = weights.tile([P, PACK, D_OUT], BF16)
+        nc.scalar.copy(out=snapped_t[:], in_=snapped_t_psum[:])
+
+        b_by_j = b_sb[:].rearrange("r (p j) -> r j p", j=PACK)
+        multiplier_t = weights_psum.tile([P, PACK, D_OUT], F32)
+        for j in range(PACK):
+            nc.tensor.matmul(
+                multiplier_t[:, j, :], lhsT=b_by_j[:, j, :], rhs=a_t[:], start=True, stop=True
+            )
+
+        w_grouped = weights.tile([P, D_OUT, PACK], BF16, align_bytes=64)
+        nc.vector.tensor_tensor(
+            out=w_grouped[:],
+            in0=multiplier_t[:].rearrange("p j o -> p o j"),
+            in1=snapped_t[:].rearrange("p j o -> p o j"),
+            op=mybir.AluOpType.mult,
+        )
+        w_codes = weights.tile([P, D_OUT], U32, align_bytes=64)
+        w_scales = weights.tile([P, D_OUT], U8, align_bytes=64)
+        nc.vector.quantize_mx(
+            out=w_codes[:].bitcast(FP8X4),
+            scales=w_scales[:],
+            in_=w_grouped[:].rearrange("p o j -> p (o j)"),
+        )
+
+        for (b, cols), raw in zip(tiles, raws):
+            grouped = stream.tile([P, N_TILE, PACK], BF16, align_bytes=64)
+            regroup(nc.vector.tensor_copy, grouped, raw, slice(0, VECTOR_COLS))
+            regroup(nc.scalar.copy, grouped, raw, slice(VECTOR_COLS, N_TILE))
+
+            x_codes = stream.tile([P, N_TILE], U32, align_bytes=64)
+            x_scales = stream.tile([P, N_TILE], U8, align_bytes=64)
+            nc.vector.quantize_mx(
+                out=x_codes[:].bitcast(FP8X4),
+                scales=x_scales[:],
+                in_=grouped[:].rearrange("p w j -> p (w j)"),
+            )
+
+            acc = acc_psum.tile([D_OUT, N_TILE], F32)
+            nc.tensor.matmul_mx(
+                out=acc[:],
+                lhsT=w_codes[:].bitcast(FP8X4),
+                lhsT_scale=w_scales[:],
+                rhs=x_codes[:].bitcast(FP8X4),
+                rhs_scale=x_scales[:],
+                start=True,
+                stop=True,
+            )
+            result = stream.tile([D_OUT, N_TILE], F32)
+            nc.scalar.copy(out=result[:], in_=acc[:])
+            nc.sync.dma_start(out=out_rows[b, :, cols], in_=result[:])

@@ -13,10 +13,16 @@ P = 128
 PACK = 4
 BATCH, CHANNELS, D_OUT, RANK, WIDTH = 2, 512, 128, 128, 1024
 N_TILE = 512
-VECTOR_COLS = N_TILE * 5 // 8
 RUN = 4
 
 FLOPS = 2 * BATCH * WIDTH * CHANNELS * D_OUT + 2 * D_OUT * RANK * CHANNELS
+
+
+def cut_into_pieces():
+    pieces = [(b, n, N_TILE) for b in range(BATCH) for n in range(0, WIDTH, N_TILE)]
+    b, n, width = pieces[-1]
+    half = width // 2
+    return pieces[:-1] + [(b, n, half), (b, n + half, half)]
 
 
 def regroup(copy, grouped, raw, cols):
@@ -32,25 +38,27 @@ def tile_ffnwithscales_pb_s_kernel(
     nc = tc.nc
     mlp_by_word = mlp.rearrange("b (p j) h w -> b p j (h w)", j=PACK)
     out_rows = out.rearrange("b o h w -> b o (h w)")
-    tiles = [(b, slice(n, n + N_TILE)) for b in range(BATCH) for n in range(0, WIDTH, N_TILE)]
+    pieces = cut_into_pieces()
+    n_pieces = len(pieces)
 
     with ExitStack() as ctx:
         weights = ctx.enter_context(tc.tile_pool(name="weights", bufs=1))
         weights_psum = ctx.enter_context(tc.psum_pool(name="weights_psum", bufs=1))
-        stream = ctx.enter_context(tc.tile_pool(name="stream", bufs=len(tiles)))
-        acc_psum = ctx.enter_context(tc.psum_pool(name="acc_psum", bufs=len(tiles)))
+        stream = ctx.enter_context(tc.tile_pool(name="stream", bufs=n_pieces))
+        acc_psum = ctx.enter_context(tc.psum_pool(name="acc_psum", bufs=n_pieces))
+        ctx.enter_context(tc.manual_schedule())
 
         a_sb = weights.tile([D_OUT, RANK], BF16)
-        nc.scalar.dma_start(out=a_sb[:], in_=down_scale_A)
+        nc.sync.dma_start(out=a_sb[:], in_=down_scale_A)
         snapped_sb = weights.tile([D_OUT, CHANNELS], BF16)
-        nc.scalar.dma_start(out=snapped_sb[:], in_=down_snapped)
+        nc.sync.dma_start(out=snapped_sb[:], in_=down_snapped)
         b_sb = weights.tile([RANK, CHANNELS], BF16)
-        nc.scalar.dma_start(out=b_sb[:], in_=down_scale_B)
+        nc.sync.dma_start(out=b_sb[:], in_=down_scale_B)
 
         raws = []
-        for b, cols in tiles:
-            raw = stream.tile([P, PACK, N_TILE], BF16)
-            nc.sync.dma_start(out=raw[:], in_=mlp_by_word[b, :, :, cols])
+        for b, n, width in pieces:
+            raw = stream.tile([P, PACK, width], BF16, name="raw")
+            nc.sync.dma_start(out=raw[:], in_=mlp_by_word[b, :, :, n : n + width])
             raws.append(raw)
 
         identity = weights.tile([P, P], BF16)
@@ -59,7 +67,7 @@ def tile_ffnwithscales_pb_s_kernel(
         a_t_psum = weights_psum.tile([RANK, D_OUT], BF16)
         nc.tensor.transpose(a_t_psum[:], a_sb[:], identity[:])
         a_t = weights.tile([RANK, D_OUT], BF16)
-        nc.vector.tensor_copy(out=a_t[:], in_=a_t_psum[:])
+        nc.scalar.copy(out=a_t[:], in_=a_t_psum[:])
 
         snapped_by_j = snapped_sb[:].rearrange("o (p j) -> o j p", j=PACK)
         snapped_t_psum = weights_psum.tile([P, PACK, D_OUT], BF16)
@@ -76,34 +84,42 @@ def tile_ffnwithscales_pb_s_kernel(
             )
 
         w_grouped = weights.tile([P, D_OUT, PACK], BF16, align_bytes=64)
-        nc.vector.tensor_tensor(
-            out=w_grouped[:],
-            in0=multiplier_t[:].rearrange("p j o -> p o j"),
-            in1=snapped_t[:].rearrange("p j o -> p o j"),
-            op=mybir.AluOpType.mult,
-        )
         w_codes = weights.tile([P, D_OUT], U32, align_bytes=64)
         w_scales = weights.tile([P, D_OUT], U8, align_bytes=64)
-        nc.vector.quantize_mx(
-            out=w_codes[:].bitcast(FP8X4),
-            scales=w_scales[:],
-            in_=w_grouped[:].rearrange("p o j -> p (o j)"),
-        )
 
-        for (b, cols), raw in zip(tiles, raws):
-            grouped = stream.tile([P, N_TILE, PACK], BF16, align_bytes=64)
-            regroup(nc.vector.tensor_copy, grouped, raw, slice(0, VECTOR_COLS))
-            regroup(nc.scalar.copy, grouped, raw, slice(VECTOR_COLS, N_TILE))
+        def quantise_weight():
+            nc.vector.tensor_tensor(
+                out=w_grouped[:],
+                in0=multiplier_t[:].rearrange("p j o -> p o j"),
+                in1=snapped_t[:].rearrange("p j o -> p o j"),
+                op=mybir.AluOpType.mult,
+            )
+            nc.vector.quantize_mx(
+                out=w_codes[:].bitcast(FP8X4),
+                scales=w_scales[:],
+                in_=w_grouped[:].rearrange("p o j -> p (o j)"),
+            )
 
-            x_codes = stream.tile([P, N_TILE], U32, align_bytes=64)
-            x_scales = stream.tile([P, N_TILE], U8, align_bytes=64)
+        groupeds, accs = [], []
+
+        def regroup_piece(i):
+            width = pieces[i][2]
+            vector_cols = width * 5 // 8
+            grouped = stream.tile([P, width, PACK], BF16, align_bytes=64, name="grouped")
+            regroup(nc.vector.tensor_copy, grouped, raws[i], slice(0, vector_cols))
+            regroup(nc.scalar.copy, grouped, raws[i], slice(vector_cols, width))
+            groupeds.append(grouped)
+
+        def quantise_and_multiply(i):
+            width = pieces[i][2]
+            x_codes = stream.tile([P, width], U32, align_bytes=64, name="x_codes")
+            x_scales = stream.tile([P, width], U8, align_bytes=64, name="x_scales")
             nc.vector.quantize_mx(
                 out=x_codes[:].bitcast(FP8X4),
                 scales=x_scales[:],
-                in_=grouped[:].rearrange("p w j -> p (w j)"),
+                in_=groupeds[i][:].rearrange("p w j -> p (w j)"),
             )
-
-            acc = acc_psum.tile([D_OUT, N_TILE], F32)
+            acc = acc_psum.tile([D_OUT, width], F32, name="acc")
             nc.tensor.matmul_mx(
                 out=acc[:],
                 lhsT=w_codes[:].bitcast(FP8X4),
@@ -113,6 +129,23 @@ def tile_ffnwithscales_pb_s_kernel(
                 start=True,
                 stop=True,
             )
-            result = stream.tile([D_OUT, N_TILE], F32)
-            nc.scalar.copy(out=result[:], in_=acc[:])
-            nc.sync.dma_start(out=out_rows[b, :, cols], in_=result[:])
+            accs.append(acc)
+
+        def copy_out_and_store(i):
+            b, n, width = pieces[i]
+            result = stream.tile([D_OUT, width], F32, name="result")
+            if i == n_pieces - 1:
+                nc.vector.tensor_copy(out=result[:], in_=accs[i][:])
+            else:
+                nc.scalar.copy(out=result[:], in_=accs[i][:])
+            nc.sync.dma_start(out=out_rows[b, :, n : n + width], in_=result[:])
+
+        for step in range(n_pieces + 2):
+            if step < n_pieces:
+                regroup_piece(step)
+            if step == 0:
+                quantise_weight()
+            if 1 <= step <= n_pieces:
+                quantise_and_multiply(step - 1)
+            if step >= 2:
+                copy_out_and_store(step - 2)

@@ -13,6 +13,7 @@ P = 128
 PACK = 4
 BATCH, CHANNELS, D_OUT, RANK, WIDTH = 2, 512, 128, 128, 1024
 N_TILE = 512
+COPY_OUT_LAG = 3
 RUN = 4
 
 FLOPS = 2 * BATCH * WIDTH * CHANNELS * D_OUT + 2 * D_OUT * RANK * CHANNELS
@@ -104,7 +105,7 @@ def tile_ffnwithscales_pb_s_kernel(
 
         def regroup_piece(i):
             width = pieces[i][2]
-            vector_cols = width * 5 // 8
+            vector_cols = width // 2
             grouped = stream.tile([P, width, PACK], BF16, align_bytes=64, name="grouped")
             regroup(nc.vector.tensor_copy, grouped, raws[i], slice(0, vector_cols))
             regroup(nc.scalar.copy, grouped, raws[i], slice(vector_cols, width))
@@ -140,12 +141,12 @@ def tile_ffnwithscales_pb_s_kernel(
                 nc.scalar.copy(out=result[:], in_=accs[i][:])
             nc.sync.dma_start(out=out_rows[b, :, n : n + width], in_=result[:])
 
-        for step in range(n_pieces + 2):
+        for step in range(n_pieces + COPY_OUT_LAG):
             if step < n_pieces:
                 regroup_piece(step)
             if step == 0:
                 quantise_weight()
             if 1 <= step <= n_pieces:
                 quantise_and_multiply(step - 1)
-            if step >= 2:
-                copy_out_and_store(step - 2)
+            if step >= COPY_OUT_LAG:
+                copy_out_and_store(step - COPY_OUT_LAG)

@@ -56,11 +56,11 @@ def tile_ffnwithscales_pb_s_kernel(
         b_sb = weights.tile([RANK, CHANNELS], BF16)
         nc.sync.dma_start(out=b_sb[:], in_=down_scale_B)
 
-        raws = []
+        raw_tiles = []
         for b, n, width in pieces:
             raw = stream.tile([P, PACK, width], BF16, name="raw")
             nc.sync.dma_start(out=raw[:], in_=mlp_by_word[b, :, :, n : n + width])
-            raws.append(raw)
+            raw_tiles.append(raw)
 
         identity = weights.tile([P, P], BF16)
         make_identity(nc, identity[:])
@@ -88,28 +88,30 @@ def tile_ffnwithscales_pb_s_kernel(
         w_codes = weights.tile([P, D_OUT], U32, align_bytes=64)
         w_scales = weights.tile([P, D_OUT], U8, align_bytes=64)
 
-        def quantise_weight():
+        def form_weight():
             nc.vector.tensor_tensor(
                 out=w_grouped[:],
                 in0=multiplier_t[:].rearrange("p j o -> p o j"),
                 in1=snapped_t[:].rearrange("p j o -> p o j"),
                 op=mybir.AluOpType.mult,
             )
+
+        def quantise_weight():
             nc.vector.quantize_mx(
                 out=w_codes[:].bitcast(FP8X4),
                 scales=w_scales[:],
                 in_=w_grouped[:].rearrange("p o j -> p (o j)"),
             )
 
-        groupeds, accs = [], []
+        grouped_tiles, acc_tiles = [], []
 
         def regroup_piece(i):
             width = pieces[i][2]
             vector_cols = width // 2
             grouped = stream.tile([P, width, PACK], BF16, align_bytes=64, name="grouped")
-            regroup(nc.vector.tensor_copy, grouped, raws[i], slice(0, vector_cols))
-            regroup(nc.scalar.copy, grouped, raws[i], slice(vector_cols, width))
-            groupeds.append(grouped)
+            regroup(nc.vector.tensor_copy, grouped, raw_tiles[i], slice(0, vector_cols))
+            regroup(nc.scalar.copy, grouped, raw_tiles[i], slice(vector_cols, width))
+            grouped_tiles.append(grouped)
 
         def quantise_and_multiply(i):
             width = pieces[i][2]
@@ -118,7 +120,7 @@ def tile_ffnwithscales_pb_s_kernel(
             nc.vector.quantize_mx(
                 out=x_codes[:].bitcast(FP8X4),
                 scales=x_scales[:],
-                in_=groupeds[i][:].rearrange("p w j -> p (w j)"),
+                in_=grouped_tiles[i][:].rearrange("p w j -> p (w j)"),
             )
             acc = acc_psum.tile([D_OUT, width], F32, name="acc")
             nc.tensor.matmul_mx(
@@ -130,21 +132,23 @@ def tile_ffnwithscales_pb_s_kernel(
                 start=True,
                 stop=True,
             )
-            accs.append(acc)
+            acc_tiles.append(acc)
 
         def copy_out_and_store(i):
             b, n, width = pieces[i]
             result = stream.tile([D_OUT, width], F32, name="result")
             if i == n_pieces - 1:
-                nc.vector.tensor_copy(out=result[:], in_=accs[i][:])
+                nc.vector.tensor_copy(out=result[:], in_=acc_tiles[i][:])
             else:
-                nc.scalar.copy(out=result[:], in_=accs[i][:])
+                nc.scalar.copy(out=result[:], in_=acc_tiles[i][:])
             nc.sync.dma_start(out=out_rows[b, :, n : n + width], in_=result[:])
 
         for step in range(n_pieces + COPY_OUT_LAG):
             if step < n_pieces:
                 regroup_piece(step)
             if step == 0:
+                form_weight()
+            if step == 1:
                 quantise_weight()
             if 1 <= step <= n_pieces:
                 quantise_and_multiply(step - 1)

@@ -137,7 +137,7 @@ def tile_ffnwithscales_pb_s_kernel(
         def copy_out_and_store(i):
             b, n, width = pieces[i]
             result = stream.tile([D_OUT, width], F32, name="result")
-            if i == n_pieces - 1:
+            if width < N_TILE:
                 nc.vector.tensor_copy(out=result[:], in_=acc_tiles[i][:])
             else:
                 nc.scalar.copy(out=result[:], in_=acc_tiles[i][:])

@@ -14,7 +14,7 @@ PACK = 4
 BATCH, CHANNELS, D_OUT, RANK, WIDTH = 2, 512, 128, 128, 1024
 N_TILE = 512
 COPY_OUT_LAG = 3
-RUN = 4
+RUN = 2
 
 FLOPS = 2 * BATCH * WIDTH * CHANNELS * D_OUT + 2 * D_OUT * RANK * CHANNELS
 

@@ -107,7 +107,7 @@ def tile_ffnwithscales_pb_s_kernel(
 
         def regroup_piece(i):
             width = pieces[i][2]
-            vector_cols = width // 2
+            vector_cols = width * 9 // 16
             grouped = stream.tile([P, width, PACK], BF16, align_bytes=64, name="grouped")
             regroup(nc.vector.tensor_copy, grouped, raw_tiles[i], slice(0, vector_cols))
             regroup(nc.scalar.copy, grouped, raw_tiles[i], slice(vector_cols, width))

@@ -16,6 +16,8 @@ N_TILE = 512
 COPY_OUT_LAG = 3
 RUN = 2
 
+KEEP_WARM = {0: 128, 1: 64}
+
 FLOPS = 2 * BATCH * WIDTH * CHANNELS * D_OUT + 2 * D_OUT * RANK * CHANNELS
 
 
@@ -65,6 +67,9 @@ def tile_ffnwithscales_pb_s_kernel(
         identity = weights.tile([P, P], BF16)
         make_identity(nc, identity[:])
 
+        zeros = weights.tile([P, P], F32)
+        nc.gpsimd.memset(zeros[:], 0.0)
+
         a_t_psum = weights_psum.tile([RANK, D_OUT], BF16)
         nc.tensor.transpose(a_t_psum[:], a_sb[:], identity[:])
         a_t = weights.tile([RANK, D_OUT], BF16)
@@ -107,7 +112,7 @@ def tile_ffnwithscales_pb_s_kernel(
 
         def regroup_piece(i):
             width = pieces[i][2]
-            vector_cols = width * 9 // 16
+            vector_cols = width * 17 // 32
             grouped = stream.tile([P, width, PACK], BF16, align_bytes=64, name="grouped")
             regroup(nc.vector.tensor_copy, grouped, raw_tiles[i], slice(0, vector_cols))
             regroup(nc.scalar.copy, grouped, raw_tiles[i], slice(vector_cols, width))
@@ -133,6 +138,14 @@ def tile_ffnwithscales_pb_s_kernel(
                 stop=True,
             )
             acc_tiles.append(acc)
+            if i in KEEP_WARM:
+                nc.tensor.matmul(
+                    multiplier_t[:, 0, : KEEP_WARM[i]],
+                    lhsT=zeros[:],
+                    rhs=zeros[:, : KEEP_WARM[i]],
+                    start=True,
+                    stop=True,
+                )
 
         def copy_out_and_store(i):
             b, n, width = pieces[i]

@@ -18,6 +18,8 @@ RUN = 2
 
 KEEP_WARM = {0: 128, 1: 64}
 
+LAST_WHOLE_PIECE = 2
+
 FLOPS = 2 * BATCH * WIDTH * CHANNELS * D_OUT + 2 * D_OUT * RANK * CHANNELS
 
 
@@ -47,7 +49,7 @@ def tile_ffnwithscales_pb_s_kernel(
     with ExitStack() as ctx:
         weights = ctx.enter_context(tc.tile_pool(name="weights", bufs=1))
         weights_psum = ctx.enter_context(tc.psum_pool(name="weights_psum", bufs=1))
-        stream = ctx.enter_context(tc.tile_pool(name="stream", bufs=n_pieces))
+        stream = ctx.enter_context(tc.tile_pool(name="stream", bufs=n_pieces + 2))
         acc_psum = ctx.enter_context(tc.psum_pool(name="acc_psum", bufs=n_pieces))
         ctx.enter_context(tc.manual_schedule())
 
@@ -112,11 +114,17 @@ def tile_ffnwithscales_pb_s_kernel(
 
         def regroup_piece(i):
             width = pieces[i][2]
-            vector_cols = width * 17 // 32
+            vector_cols = width // 2 if width == N_TILE else width * 11 // 16
             grouped = stream.tile([P, width, PACK], BF16, align_bytes=64, name="grouped")
             regroup(nc.vector.tensor_copy, grouped, raw_tiles[i], slice(0, vector_cols))
             regroup(nc.scalar.copy, grouped, raw_tiles[i], slice(vector_cols, width))
             grouped_tiles.append(grouped)
+
+        def parts_of(i):
+            width = pieces[i][2]
+            if i < n_pieces - 1:
+                return [slice(0, width)]
+            return [slice(0, width // 2), slice(width // 2, width)]
 
         def quantise_and_multiply(i):
             width = pieces[i][2]
@@ -127,17 +135,20 @@ def tile_ffnwithscales_pb_s_kernel(
                 scales=x_scales[:],
                 in_=grouped_tiles[i][:].rearrange("p w j -> p (w j)"),
             )
-            acc = acc_psum.tile([D_OUT, width], F32, name="acc")
-            nc.tensor.matmul_mx(
-                out=acc[:],
-                lhsT=w_codes[:].bitcast(FP8X4),
-                lhsT_scale=w_scales[:],
-                rhs=x_codes[:].bitcast(FP8X4),
-                rhs_scale=x_scales[:],
-                start=True,
-                stop=True,
-            )
-            acc_tiles.append(acc)
+            acc_of_piece = []
+            for cols in parts_of(i):
+                acc = acc_psum.tile([D_OUT, cols.stop - cols.start], F32, name="acc")
+                nc.tensor.matmul_mx(
+                    out=acc[:],
+                    lhsT=w_codes[:].bitcast(FP8X4),
+                    lhsT_scale=w_scales[:],
+                    rhs=x_codes[:, cols].bitcast(FP8X4),
+                    rhs_scale=x_scales[:, cols],
+                    start=True,
+                    stop=True,
+                )
+                acc_of_piece.append(acc)
+            acc_tiles.append(acc_of_piece)
             if i in KEEP_WARM:
                 nc.tensor.matmul(
                     multiplier_t[:, 0, : KEEP_WARM[i]],
@@ -149,12 +160,17 @@ def tile_ffnwithscales_pb_s_kernel(
 
         def copy_out_and_store(i):
             b, n, width = pieces[i]
-            result = stream.tile([D_OUT, width], F32, name="result")
-            if width < N_TILE:
-                nc.vector.tensor_copy(out=result[:], in_=acc_tiles[i][:])
-            else:
-                nc.scalar.copy(out=result[:], in_=acc_tiles[i][:])
-            nc.sync.dma_start(out=out_rows[b, :, n : n + width], in_=result[:])
+            store_cols = width // 2 if i == LAST_WHOLE_PIECE else width
+            for part, cols in enumerate(parts_of(i)):
+                copy = nc.vector.tensor_copy if width < N_TILE and part == 0 else nc.scalar.copy
+                acc = acc_tiles[i][part]
+                part_cols = cols.stop - cols.start
+                step = min(store_cols, part_cols)
+                for m in range(0, part_cols, step):
+                    result = stream.tile([D_OUT, step], F32, name="result")
+                    copy(out=result[:], in_=acc[:, m : m + step])
+                    first = n + cols.start + m
+                    nc.sync.dma_start(out=out_rows[b, :, first : first + step], in_=result[:])
 
         for step in range(n_pieces + COPY_OUT_LAG):
             if step < n_pieces:

from contextlib import ExitStack

import concourse.mybir as mybir
from concourse.masks import make_identity

BF16 = mybir.dt.bfloat16
F32 = mybir.dt.float32
U32 = mybir.dt.uint32
U8 = mybir.dt.uint8
FP8X4 = mybir.dt.float8_e4m3fn_x4

P = 128
PACK = 4
BATCH, CHANNELS, D_OUT, RANK, WIDTH = 2, 512, 128, 128, 1024
N_TILE = 512
COPY_OUT_LAG = 3
RUN = 2

KEEP_WARM = {0: 128, 1: 64}

LAST_WHOLE_PIECE = 2

FLOPS = 2 * BATCH * WIDTH * CHANNELS * D_OUT + 2 * D_OUT * RANK * CHANNELS


def cut_into_pieces():
    pieces = [(b, n, N_TILE) for b in range(BATCH) for n in range(0, WIDTH, N_TILE)]
    b, n, width = pieces[-1]
    half = width // 2
    return pieces[:-1] + [(b, n, half), (b, n + half, half)]


def regroup(copy, grouped, raw, cols):
    copy(
        out=grouped[:, cols, :].rearrange("p (c i) j -> p c j i", i=RUN),
        in_=raw[:, :, cols].rearrange("p j (c i) -> p c j i", i=RUN),
    )


def tile_ffnwithscales_pb_s_kernel(
    tc, mlp, down_snapped, down_scale_A, down_scale_B, out
):
    nc = tc.nc
    mlp_by_word = mlp.rearrange("b (p j) h w -> b p j (h w)", j=PACK)
    out_rows = out.rearrange("b o h w -> b o (h w)")
    pieces = cut_into_pieces()
    n_pieces = len(pieces)

    with ExitStack() as ctx:
        weights = ctx.enter_context(tc.tile_pool(name="weights", bufs=1))
        weights_psum = ctx.enter_context(tc.psum_pool(name="weights_psum", bufs=1))
        stream = ctx.enter_context(tc.tile_pool(name="stream", bufs=n_pieces + 2))
        acc_psum = ctx.enter_context(tc.psum_pool(name="acc_psum", bufs=n_pieces))
        ctx.enter_context(tc.manual_schedule())

        a_sb = weights.tile([D_OUT, RANK], BF16)
        nc.sync.dma_start(out=a_sb[:], in_=down_scale_A)
        snapped_sb = weights.tile([D_OUT, CHANNELS], BF16)
        nc.sync.dma_start(out=snapped_sb[:], in_=down_snapped)
        b_sb = weights.tile([RANK, CHANNELS], BF16)
        nc.sync.dma_start(out=b_sb[:], in_=down_scale_B)

        raw_tiles = []
        for b, n, width in pieces:
            raw = stream.tile([P, PACK, width], BF16, name="raw")
            nc.sync.dma_start(out=raw[:], in_=mlp_by_word[b, :, :, n : n + width])
            raw_tiles.append(raw)

        identity = weights.tile([P, P], BF16)
        make_identity(nc, identity[:])

        zeros = weights.tile([P, P], F32)
        nc.gpsimd.memset(zeros[:], 0.0)

        a_t_psum = weights_psum.tile([RANK, D_OUT], BF16)
        nc.tensor.transpose(a_t_psum[:], a_sb[:], identity[:])
        a_t = weights.tile([RANK, D_OUT], BF16)
        nc.scalar.copy(out=a_t[:], in_=a_t_psum[:])

        snapped_by_j = snapped_sb[:].rearrange("o (p j) -> o j p", j=PACK)
        snapped_t_psum = weights_psum.tile([P, PACK, D_OUT], BF16)
        for j in range(PACK):
            nc.tensor.transpose(snapped_t_psum[:, j, :], snapped_by_j[:, j, :], identity[:])
        snapped_t = weights.tile([P, PACK, D_OUT], BF16)
        nc.scalar.copy(out=snapped_t[:], in_=snapped_t_psum[:])

        b_by_j = b_sb[:].rearrange("r (p j) -> r j p", j=PACK)
        multiplier_t = weights_psum.tile([P, PACK, D_OUT], F32)
        for j in range(PACK):
            nc.tensor.matmul(
                multiplier_t[:, j, :], lhsT=b_by_j[:, j, :], rhs=a_t[:], start=True, stop=True
            )

        w_grouped = weights.tile([P, D_OUT, PACK], BF16, align_bytes=64)
        w_codes = weights.tile([P, D_OUT], U32, align_bytes=64)
        w_scales = weights.tile([P, D_OUT], U8, align_bytes=64)

        def form_weight():
            nc.vector.tensor_tensor(
                out=w_grouped[:],
                in0=multiplier_t[:].rearrange("p j o -> p o j"),
                in1=snapped_t[:].rearrange("p j o -> p o j"),
                op=mybir.AluOpType.mult,
            )

        def quantise_weight():
            nc.vector.quantize_mx(
                out=w_codes[:].bitcast(FP8X4),
                scales=w_scales[:],
                in_=w_grouped[:].rearrange("p o j -> p (o j)"),
            )

        grouped_tiles, acc_tiles = [], []

        def regroup_piece(i):
            width = pieces[i][2]
            vector_cols = width // 2 if width == N_TILE else width * 11 // 16
            grouped = stream.tile([P, width, PACK], BF16, align_bytes=64, name="grouped")
            regroup(nc.vector.tensor_copy, grouped, raw_tiles[i], slice(0, vector_cols))
            regroup(nc.scalar.copy, grouped, raw_tiles[i], slice(vector_cols, width))
            grouped_tiles.append(grouped)

        def parts_of(i):
            width = pieces[i][2]
            if i < n_pieces - 1:
                return [slice(0, width)]
            return [slice(0, width // 2), slice(width // 2, width)]

        def quantise_and_multiply(i):
            width = pieces[i][2]
            x_codes = stream.tile([P, width], U32, align_bytes=64, name="x_codes")
            x_scales = stream.tile([P, width], U8, align_bytes=64, name="x_scales")
            nc.vector.quantize_mx(
                out=x_codes[:].bitcast(FP8X4),
                scales=x_scales[:],
                in_=grouped_tiles[i][:].rearrange("p w j -> p (w j)"),
            )
            acc_of_piece = []
            for cols in parts_of(i):
                acc = acc_psum.tile([D_OUT, cols.stop - cols.start], F32, name="acc")
                nc.tensor.matmul_mx(
                    out=acc[:],
                    lhsT=w_codes[:].bitcast(FP8X4),
                    lhsT_scale=w_scales[:],
                    rhs=x_codes[:, cols].bitcast(FP8X4),
                    rhs_scale=x_scales[:, cols],
                    start=True,
                    stop=True,
                )
                acc_of_piece.append(acc)
            acc_tiles.append(acc_of_piece)
            if i in KEEP_WARM:
                nc.tensor.matmul(
                    multiplier_t[:, 0, : KEEP_WARM[i]],
                    lhsT=zeros[:],
                    rhs=zeros[:, : KEEP_WARM[i]],
                    start=True,
                    stop=True,
                )

        def copy_out_and_store(i):
            b, n, width = pieces[i]
            store_cols = width // 2 if i == LAST_WHOLE_PIECE else width
            for part, cols in enumerate(parts_of(i)):
                copy = nc.vector.tensor_copy if width < N_TILE and part == 0 else nc.scalar.copy
                acc = acc_tiles[i][part]
                part_cols = cols.stop - cols.start
                step = min(store_cols, part_cols)
                for m in range(0, part_cols, step):
                    result = stream.tile([D_OUT, step], F32, name="result")
                    copy(out=result[:], in_=acc[:, m : m + step])
                    first = n + cols.start + m
                    nc.sync.dma_start(out=out_rows[b, :, first : first + step], in_=result[:])

        for step in range(n_pieces + COPY_OUT_LAG):
            if step < n_pieces:
                regroup_piece(step)
            if step == 0:
                form_weight()
            if step == 1:
                quantise_weight()
            if 1 <= step <= n_pieces:
                quantise_and_multiply(step - 1)
            if step >= COPY_OUT_LAG:
                copy_out_and_store(step - COPY_OUT_LAG)
